import numpy as np
import ml_dtypes


def mxq(x, axis, fmt="e4m3"):
    dtype, down = {"e4m3": (ml_dtypes.float8_e4m3fn, 7), "e5m2": (ml_dtypes.float8_e5m2, 14)}[fmt]
    v = np.moveaxis(np.asarray(x, np.float32).astype(ml_dtypes.bfloat16).astype(np.float64), axis, -1)
    blocks = v.reshape(v.shape[:-1] + (-1, 32))
    amax = np.abs(blocks).max(-1, keepdims=True)
    byte = np.maximum(np.where(amax > 0, np.frexp(amax)[1] - 1 + 127, 0) - down, 1)
    scale = np.exp2(byte - 127.0)
    codes = (blocks / scale).astype(np.float32).astype(dtype).astype(np.float64)
    return np.moveaxis((codes * scale).reshape(v.shape), -1, axis)


WIDE = False


def mx_kscale(k):
    if not WIDE:
        return np.ones(k)
    levels = np.array([10, -10, 5, -5, 0])
    a = np.random.permutation(np.resize(levels, k // 512 * 4)).reshape(k // 512, 4)
    idx = np.arange(k)
    return np.exp2(a[idx // 512, idx % 128 // 32])


BF16 = ml_dtypes.bfloat16


def bf(x):
    return np.asarray(x, np.float32).astype(BF16)


def f64(x):
    return np.asarray(x).astype(np.float64)


E2M1 = np.array([0.0, 0.5, 1.0, 1.5, 2.0, 3.0, 4.0, 6.0, -0.0, -0.5, -1.0, -1.5, -2.0, -3.0, -4.0, -6.0])


def pack_weight(w, fmt):
    k, n = w.shape
    w = f64(bf(w)).reshape(k // 32, 32, n)
    amax = np.abs(w).max(1)
    if fmt == "e4m3":
        byte = np.frexp(amax)[1] - 1 + 127 - 7
    else:
        mant, ex = np.frexp(amax / 6.0)
        byte = np.where(mant > 0.5, ex, ex - 1) + 127
    byte = np.clip(np.where(amax > 0, byte, 1), 1, 254)
    scaled = (w * np.exp2(127.0 - byte)[:, None, :]).reshape(k, n).astype(np.float32)
    by_word = np.ascontiguousarray(scaled.reshape(k // 512, 128, 4, n).transpose(0, 1, 3, 2))
    if fmt == "e4m3":
        words = by_word.astype(ml_dtypes.float8_e4m3fn).view(np.uint8)
    else:
        c = by_word.astype(ml_dtypes.float4_e2m1fn).view(np.uint8) & 0xF
        words = c[..., 0::2] | (c[..., 1::2] << 4)
    return np.ascontiguousarray(words), np.ascontiguousarray(byte.astype(np.uint8).reshape(k // 512, 16, n))


def unpack_weight(words, scales, fmt):
    g, p, n, _ = words.shape
    if fmt == "e4m3":
        vals = np.ascontiguousarray(words).view(ml_dtypes.float8_e4m3fn).astype(np.float64)
    else:
        nib = np.empty((g, p, n, 4), np.uint8)
        nib[..., 0::2] = words & 0xF
        nib[..., 1::2] = words >> 4
        vals = E2M1[nib]
    vals = vals * np.repeat(np.exp2(scales.astype(np.float64) - 127.0), 8, axis=1)[..., None]
    return vals.transpose(0, 1, 3, 2).reshape(g * 512, n)


B, IMG, P0, P1, C, F = 8, 256, 16, 64, 4, 1024
E0, E1 = IMG // P0, IMG // P1
N0, N1 = E0 * E0, E1 * E1
D0, D1 = P0 * P0 * C, P1 * P1 * C


def setup_inputs():
    s = mx_kscale(D1)
    flat = np.random.standard_normal((B, N1, D1)) * s
    img = flat.reshape(B, E1, E1, P1, P1, C).transpose(0, 1, 3, 2, 4, 5).reshape(B, IMG, IMG, C)
    encoded = img.reshape(B, E0, P0, E0, P0, C).transpose(0, 1, 3, 2, 4, 5).reshape(B, N0, D0)
    words, scales = pack_weight(np.random.standard_normal((D1, F)) / np.sqrt(D1) / s[:, None], "e4m3")
    return {"encoded": bf(encoded),
            "W_words": words,
            "W_scales": scales,
            "b": bf(np.random.standard_normal(F) * 0.3),
            "pos_emb": bf(np.random.standard_normal((N1, F)) * 0.5)}


def reference(encoded, W_words, W_scales, b, pos_emb):
    x = f64(encoded).reshape(-1, E0, E0, P0, P0, C)
    img = x.transpose(0, 1, 3, 2, 4, 5).reshape(-1, IMG, IMG, C)
    new_patches = img.reshape(-1, E1, P1, E1, P1, C).transpose(0, 1, 3, 2, 4, 5)
    flat = new_patches.reshape(-1, N1, D1)
    return (mxq(flat, 2, "e4m3") @ unpack_weight(W_words, W_scales, "e4m3")) + f64(b) + f64(pos_emb)

@@ -1,0 +1,139 @@
+import concourse.mybir as mybir
+from concourse.masks import make_identity
+
+F32 = mybir.dt.float32
+BF16 = mybir.dt.bfloat16
+I32 = mybir.dt.int32
+U32 = mybir.dt.uint32
+U8 = mybir.dt.uint8
+FP8X4 = mybir.dt.float8_e4m3fn_x4
+ADD = mybir.AluOpType.add
+
+P = 128
+IMAGES = 8
+BIG_PATCHES = 16
+F = 1024
+K = 16384
+K_PASS = 512
+PASSES = K // K_PASS
+N_TILE = 512
+N_TILES = F // N_TILE
+SLABS = 4
+SLAB_PASSES = PASSES // SLABS
+SLAB_COLS = K // SLABS
+PASSES_PER_LOAD = 2
+PLANES_PER_TILE = 4
+PLANE_SETS = PASSES // PLANES_PER_TILE
+
+FLOPS = 2 * P * K * F
+
+
+def tile_resampling_k_kernel(tc, encoded, W_words, W_scales, b, pos_emb, out):
+    nc = tc.nc
+    with (
+        tc.tile_pool(name="const", bufs=1) as const,
+        tc.tile_pool(name="raw", bufs=SLABS) as raw_pool,
+        tc.tile_pool(name="stage", bufs=2) as stage,
+        tc.tile_pool(name="weights", bufs=PASSES // PASSES_PER_LOAD) as weights,
+        tc.psum_pool(name="acc", bufs=1) as acc_pool,
+        tc.psum_pool(name="turned", bufs=4) as turned_pool,
+        tc.psum_pool(name="addend_ps", bufs=2) as addend_pool,
+    ):
+        ident = const.tile([P, P], F32)
+        make_identity(nc, ident[:])
+        planes = const.tile([P, PLANE_SETS, F], U8, align_bytes=64)
+        nc.vector.memset(planes[:].bitcast(I32), 0)
+        table = const.tile([P, F], BF16)
+        nc.vector.memset(table[:], 0.0)
+
+        by_slab = encoded.rearrange("i (y a x c) d -> a (i y) x (c d)", y=4, a=SLABS, x=4, c=4)
+        raws = []
+        for a in range(SLABS):
+            raw = raw_pool.tile([P, 4, 16, 64], BF16)
+            nc.sync.dma_start(out=raw[:].rearrange("p c r w -> p (c r w)"), in_=by_slab[a])
+            raws.append(raw)
+        nc.sync.dma_start(out=table[0:BIG_PATCHES, :], in_=pos_emb)
+        nc.sync.dma_start(out=table[BIG_PATCHES : BIG_PATCHES + 1, :], in_=b.unsqueeze(0))
+        for G in range(PLANE_SETS):
+            for Q in range(4):
+                nc.sync.dma_start(
+                    out=planes[32 * Q : 32 * Q + 16, G, :].bitcast(I32),
+                    in_=W_scales[4 * G : 4 * G + 4, 4 * Q : 4 * Q + 4, :].bitcast(I32),
+                )
+        w_tiles = []
+        for g0 in range(0, PASSES, PASSES_PER_LOAD):
+            w = weights.tile([P, PASSES_PER_LOAD, F], U32, align_bytes=64)
+            nc.sync.dma_start(
+                out=w[:].bitcast(I32),
+                in_=W_words[g0 : g0 + PASSES_PER_LOAD].rearrange("g p n t -> p g (n t)").bitcast(I32),
+            )
+            w_tiles.append(w)
+
+        select = const.tile([P, IMAGES, BIG_PATCHES], BF16)
+        nc.vector.tensor_scalar(
+            out=select[:],
+            in0=ident[:, 0:BIG_PATCHES].unsqueeze(1).to_broadcast([P, IMAGES, BIG_PATCHES]),
+            scalar1=ident[:, BIG_PATCHES : BIG_PATCHES + 1],
+            scalar2=None,
+            op0=ADD,
+        )
+        addend = const.tile([P, F], F32)
+        for h in range(N_TILES):
+            cols = slice(h * N_TILE, (h + 1) * N_TILE)
+            addend_ps = addend_pool.tile([P, N_TILE], F32)
+            nc.tensor.matmul(
+                out=addend_ps[:],
+                lhsT=select[:].rearrange("p i j -> p (i j)"),
+                rhs=table[:, cols],
+                start=True,
+                stop=True,
+            )
+            nc.scalar.copy(out=addend[:, cols], in_=addend_ps[:])
+
+        x_codes = const.tile([P, PASSES, P], U32, align_bytes=64)
+        x_scales = const.tile([P, PASSES, P], U8, align_bytes=64)
+        for a in range(SLABS):
+            ordered = stage.tile([P, 16, 4, 64], BF16)
+            nc.vector.tensor_copy(out=ordered[:], in_=raws[a][:].rearrange("p c r w -> p r c w"))
+            words = ordered[:].rearrange("p r c w -> p (r c w)").bitcast(F32)
+            grouped = stage.tile([P, SLAB_PASSES, P, 4], BF16, align_bytes=64)
+            grouped_words = grouped[:].bitcast(F32)
+            for pair in range(SLAB_PASSES // 2):
+                turned = turned_pool.tile([P, 2, 2, P], F32)
+                for j in range(2):
+                    first = 256 * (2 * pair + j)
+                    for u in range(2):
+                        nc.tensor.transpose(turned[:, j, u, :], words[:, first + u : first + 256 : 2], ident[:])
+                nc.scalar.copy(
+                    out=grouped_words[:, 2 * pair : 2 * pair + 2, :, :],
+                    in_=turned[:].rearrange("p j u m -> p j m u"),
+                )
+            slab = slice(a * SLAB_PASSES, (a + 1) * SLAB_PASSES)
+            nc.vector.quantize_mx(
+                out=x_codes[:, slab, :].rearrange("p g m -> p (g m)").bitcast(FP8X4),
+                scales=x_scales[:, slab, :].rearrange("p g m -> p (g m)"),
+                in_=grouped[:].rearrange("p g m t -> p (g m t)"),
+            )
+
+        accs = [acc_pool.tile([P, N_TILE], F32, name="acc%d" % h) for h in range(N_TILES)]
+        for g in range(PASSES):
+            w = w_tiles[g // PASSES_PER_LOAD]
+            first_row = 4 * (g % PLANES_PER_TILE)
+            for h in range(N_TILES):
+                cols = slice(h * N_TILE, (h + 1) * N_TILE)
+                nc.tensor.matmul_mx(
+                    out=accs[h][:],
+                    lhsT=x_codes[:, g, :].bitcast(FP8X4),
+                    lhsT_scale=x_scales[:, g, :],
+                    rhs=w[:, g % PASSES_PER_LOAD, cols].bitcast(FP8X4),
+                    rhs_scale=planes[first_row:P, g // PLANES_PER_TILE, cols],
+                    start=(g == 0),
+                    stop=(g == PASSES - 1),
+                )
+
+        out_rows = out.flatten_outer_dims()
+        result = const.tile([P, F], F32)
+        for h in range(N_TILES):
+            cols = slice(h * N_TILE, (h + 1) * N_TILE)
+            nc.vector.tensor_tensor(out=result[:, cols], in0=accs[h][:], in1=addend[:, cols], op=ADD)
+            nc.sync.dma_start(out=out_rows[:, cols], in_=result[:, cols])

@@ -56,9 +56,9 @@ def tile_resampling_k_kernel(tc, encoded, W_words, W_scales, b, pos_emb, out):
         nc.sync.dma_start(out=table[BIG_PATCHES : BIG_PATCHES + 1, :], in_=b.unsqueeze(0))
         for G in range(PLANE_SETS):
             for Q in range(4):
-                nc.sync.dma_start(
-                    out=planes[32 * Q : 32 * Q + 16, G, :].bitcast(I32),
-                    in_=W_scales[4 * G : 4 * G + 4, 4 * Q : 4 * Q + 4, :].bitcast(I32),
+                nc.gpsimd.dma_start(
+                    out=planes[32 * Q : 32 * Q + 16, G, :].bitcast(F32),
+                    in_=W_scales[4 * G : 4 * G + 4, 4 * Q : 4 * Q + 4, :].bitcast(F32),
                 )
         w_tiles = []
         for g0 in range(0, PASSES, PASSES_PER_LOAD):

@@ -22,8 +22,10 @@ SLABS = 4
 SLAB_PASSES = PASSES // SLABS
 SLAB_COLS = K // SLABS
 PASSES_PER_LOAD = 2
-PLANES_PER_TILE = 4
-PLANE_SETS = PASSES // PLANES_PER_TILE
+TAIL_PASSES = 2
+MAIN_PASSES = PASSES - TAIL_PASSES
+PLANE_STARTS = 4
+PLANE_SETS = PASSES // PLANE_STARTS
 
 FLOPS = 2 * P * K * F
 
@@ -34,7 +36,8 @@ def tile_resampling_k_kernel(tc, encoded, W_words, W_scales, b, pos_emb, out):
         tc.tile_pool(name="const", bufs=1) as const,
         tc.tile_pool(name="raw", bufs=SLABS) as raw_pool,
         tc.tile_pool(name="stage", bufs=2) as stage,
-        tc.tile_pool(name="weights", bufs=PASSES // PASSES_PER_LOAD) as weights,
+        tc.tile_pool(name="weights", bufs=MAIN_PASSES // PASSES_PER_LOAD) as weights,
+        tc.tile_pool(name="tail", bufs=TAIL_PASSES * N_TILES) as tail_pool,
         tc.psum_pool(name="acc", bufs=1) as acc_pool,
         tc.psum_pool(name="turned", bufs=4) as turned_pool,
         tc.psum_pool(name="addend_ps", bufs=2) as addend_pool,
@@ -61,13 +64,22 @@ def tile_resampling_k_kernel(tc, encoded, W_words, W_scales, b, pos_emb, out):
                     in_=W_scales[4 * G : 4 * G + 4, 4 * Q : 4 * Q + 4, :].bitcast(F32),
                 )
         w_tiles = []
-        for g0 in range(0, PASSES, PASSES_PER_LOAD):
+        for g0 in range(0, MAIN_PASSES, PASSES_PER_LOAD):
             w = weights.tile([P, PASSES_PER_LOAD, F], U32, align_bytes=64)
             nc.sync.dma_start(
                 out=w[:].bitcast(I32),
                 in_=W_words[g0 : g0 + PASSES_PER_LOAD].rearrange("g p n t -> p g (n t)").bitcast(I32),
             )
             w_tiles.append(w)
+        tail_tiles = {}
+        for h in range(N_TILES):
+            for g in range(MAIN_PASSES, PASSES):
+                w_tail = tail_pool.tile([P, N_TILE], U32, align_bytes=64)
+                nc.sync.dma_start(
+                    out=w_tail[:].bitcast(I32),
+                    in_=W_words[g].rearrange("p n t -> p (n t)").bitcast(I32)[:, h * N_TILE : (h + 1) * N_TILE],
+                )
+                tail_tiles[(g, h)] = w_tail
 
         select = const.tile([P, IMAGES, BIG_PATCHES], BF16)
         nc.vector.tensor_scalar(
@@ -94,7 +106,7 @@ def tile_resampling_k_kernel(tc, encoded, W_words, W_scales, b, pos_emb, out):
         x_scales = const.tile([P, PASSES, P], U8, align_bytes=64)
         for a in range(SLABS):
             ordered = stage.tile([P, 16, 4, 64], BF16)
-            nc.vector.tensor_copy(out=ordered[:], in_=raws[a][:].rearrange("p c r w -> p r c w"))
+            nc.scalar.copy(out=ordered[:].bitcast(F32), in_=raws[a][:].bitcast(F32).rearrange("p c r w -> p r c w"))
             words = ordered[:].rearrange("p r c w -> p (r c w)").bitcast(F32)
             grouped = stage.tile([P, SLAB_PASSES, P, 4], BF16, align_bytes=64)
             grouped_words = grouped[:].bitcast(F32)
@@ -104,7 +116,7 @@ def tile_resampling_k_kernel(tc, encoded, W_words, W_scales, b, pos_emb, out):
                     first = 256 * (2 * pair + j)
                     for u in range(2):
                         nc.tensor.transpose(turned[:, j, u, :], words[:, first + u : first + 256 : 2], ident[:])
-                nc.scalar.copy(
+                nc.vector.tensor_copy(
                     out=grouped_words[:, 2 * pair : 2 * pair + 2, :, :],
                     in_=turned[:].rearrange("p j u m -> p j m u"),
                 )
@@ -116,24 +128,27 @@ def tile_resampling_k_kernel(tc, encoded, W_words, W_scales, b, pos_emb, out):
             )
 
         accs = [acc_pool.tile([P, N_TILE], F32, name="acc%d" % h) for h in range(N_TILES)]
-        for g in range(PASSES):
-            w = w_tiles[g // PASSES_PER_LOAD]
-            first_row = 4 * (g % PLANES_PER_TILE)
+
+        def mx_pass(g, h, w_words):
+            nc.tensor.matmul_mx(
+                out=accs[h][:],
+                lhsT=x_codes[:, g, :].bitcast(FP8X4),
+                lhsT_scale=x_scales[:, g, :],
+                rhs=w_words.bitcast(FP8X4),
+                rhs_scale=planes[4 * (g % PLANE_STARTS) : P, g // PLANE_STARTS, h * N_TILE : (h + 1) * N_TILE],
+                start=(g == 0),
+                stop=(g == PASSES - 1),
+            )
+
+        for g in range(MAIN_PASSES):
             for h in range(N_TILES):
-                cols = slice(h * N_TILE, (h + 1) * N_TILE)
-                nc.tensor.matmul_mx(
-                    out=accs[h][:],
-                    lhsT=x_codes[:, g, :].bitcast(FP8X4),
-                    lhsT_scale=x_scales[:, g, :],
-                    rhs=w[:, g % PASSES_PER_LOAD, cols].bitcast(FP8X4),
-                    rhs_scale=planes[first_row:P, g // PLANES_PER_TILE, cols],
-                    start=(g == 0),
-                    stop=(g == PASSES - 1),
-                )
+                mx_pass(g, h, w_tiles[g // PASSES_PER_LOAD][:, g % PASSES_PER_LOAD, h * N_TILE : (h + 1) * N_TILE])
 
         out_rows = out.flatten_outer_dims()
         result = const.tile([P, F], F32)
         for h in range(N_TILES):
             cols = slice(h * N_TILE, (h + 1) * N_TILE)
+            for g in range(MAIN_PASSES, PASSES):
+                mx_pass(g, h, tail_tiles[(g, h)][:])
             nc.vector.tensor_tensor(out=result[:, cols], in0=accs[h][:], in1=addend[:, cols], op=ADD)
             nc.sync.dma_start(out=out_rows[:, cols], in_=result[:, cols])

@@ -18,6 +18,9 @@ K_PASS = 512
 PASSES = K // K_PASS
 N_TILE = 512
 N_TILES = F // N_TILE
+BLOCKS = ((0, 512), (512, 256), (768, 128), (896, 128))
+LEFT = BLOCKS[0]
+RIGHT = BLOCKS[1:]
 SLABS = 4
 SLAB_PASSES = PASSES // SLABS
 SLAB_COLS = K // SLABS
@@ -37,10 +40,9 @@ def tile_resampling_k_kernel(tc, encoded, W_words, W_scales, b, pos_emb, out):
         tc.tile_pool(name="raw", bufs=SLABS) as raw_pool,
         tc.tile_pool(name="stage", bufs=2) as stage,
         tc.tile_pool(name="weights", bufs=MAIN_PASSES // PASSES_PER_LOAD) as weights,
-        tc.tile_pool(name="tail", bufs=TAIL_PASSES * N_TILES) as tail_pool,
+        tc.tile_pool(name="tail", bufs=1) as tail_pool,
         tc.psum_pool(name="acc", bufs=1) as acc_pool,
         tc.psum_pool(name="turned", bufs=4) as turned_pool,
-        tc.psum_pool(name="addend_ps", bufs=2) as addend_pool,
     ):
         ident = const.tile([P, P], F32)
         make_identity(nc, ident[:])
@@ -71,15 +73,17 @@ def tile_resampling_k_kernel(tc, encoded, W_words, W_scales, b, pos_emb, out):
                 in_=W_words[g0 : g0 + PASSES_PER_LOAD].rearrange("g p n t -> p g (n t)").bitcast(I32),
             )
             w_tiles.append(w)
-        tail_tiles = {}
-        for h in range(N_TILES):
-            for g in range(MAIN_PASSES, PASSES):
-                w_tail = tail_pool.tile([P, N_TILE], U32, align_bytes=64)
-                nc.sync.dma_start(
-                    out=w_tail[:].bitcast(I32),
-                    in_=W_words[g].rearrange("p n t -> p (n t)").bitcast(I32)[:, h * N_TILE : (h + 1) * N_TILE],
-                )
-                tail_tiles[(g, h)] = w_tail
+        def load_tail(g, first, width):
+            w_tail = tail_pool.tile([P, width], U32, align_bytes=64, name="tail_%d_%d" % (g, first))
+            nc.sync.dma_start(
+                out=w_tail[:].bitcast(I32),
+                in_=W_words[g].rearrange("p n t -> p (n t)").bitcast(I32)[:, first : first + width],
+            )
+            return w_tail
+
+        left_tails = [load_tail(g, LEFT[0], LEFT[1]) for g in range(MAIN_PASSES, PASSES)]
+        right_before_last = load_tail(PASSES - 2, N_TILE, N_TILE)
+        right_last = [load_tail(PASSES - 1, first, width) for first, width in RIGHT]
 
         select = const.tile([P, IMAGES, BIG_PATCHES], BF16)
         nc.vector.tensor_scalar(
@@ -92,15 +96,15 @@ def tile_resampling_k_kernel(tc, encoded, W_words, W_scales, b, pos_emb, out):
         addend = const.tile([P, F], F32)
         for h in range(N_TILES):
             cols = slice(h * N_TILE, (h + 1) * N_TILE)
-            addend_ps = addend_pool.tile([P, N_TILE], F32)
+            turned = turned_pool.tile([P, N_TILE], F32)
             nc.tensor.matmul(
-                out=addend_ps[:],
+                out=turned[:],
                 lhsT=select[:].rearrange("p i j -> p (i j)"),
                 rhs=table[:, cols],
                 start=True,
                 stop=True,
             )
-            nc.scalar.copy(out=addend[:, cols], in_=addend_ps[:])
+            nc.scalar.copy(out=addend[:, cols], in_=turned[:])
 
         x_codes = const.tile([P, PASSES, P], U32, align_bytes=64)
         x_scales = const.tile([P, PASSES, P], U8, align_bytes=64)
@@ -127,28 +131,39 @@ def tile_resampling_k_kernel(tc, encoded, W_words, W_scales, b, pos_emb, out):
                 in_=grouped[:].rearrange("p g m t -> p (g m t)"),
             )
 
-        accs = [acc_pool.tile([P, N_TILE], F32, name="acc%d" % h) for h in range(N_TILES)]
+        accs = [acc_pool.tile([P, width], F32, name="acc%d" % first) for first, width in BLOCKS]
 
-        def mx_pass(g, h, w_words):
+        def mx_pass(g, block, w_words):
+            first, width = BLOCKS[block]
             nc.tensor.matmul_mx(
-                out=accs[h][:],
+                out=accs[block][:],
                 lhsT=x_codes[:, g, :].bitcast(FP8X4),
                 lhsT_scale=x_scales[:, g, :],
                 rhs=w_words.bitcast(FP8X4),
-                rhs_scale=planes[4 * (g % PLANE_STARTS) : P, g // PLANE_STARTS, h * N_TILE : (h + 1) * N_TILE],
+                rhs_scale=planes[4 * (g % PLANE_STARTS) : P, g // PLANE_STARTS, first : first + width],
                 start=(g == 0),
                 stop=(g == PASSES - 1),
             )
 
         for g in range(MAIN_PASSES):
-            for h in range(N_TILES):
-                mx_pass(g, h, w_tiles[g // PASSES_PER_LOAD][:, g % PASSES_PER_LOAD, h * N_TILE : (h + 1) * N_TILE])
+            for block, (first, width) in enumerate(BLOCKS):
+                mx_pass(g, block, w_tiles[g // PASSES_PER_LOAD][:, g % PASSES_PER_LOAD, first : first + width])
 
         out_rows = out.flatten_outer_dims()
         result = const.tile([P, F], F32)
-        for h in range(N_TILES):
-            cols = slice(h * N_TILE, (h + 1) * N_TILE)
-            for g in range(MAIN_PASSES, PASSES):
-                mx_pass(g, h, tail_tiles[(g, h)][:])
-            nc.vector.tensor_tensor(out=result[:, cols], in0=accs[h][:], in1=addend[:, cols], op=ADD)
+
+        def finish(block):
+            first, width = BLOCKS[block]
+            cols = slice(first, first + width)
+            nc.vector.tensor_tensor(out=result[:, cols], in0=accs[block][:], in1=addend[:, cols], op=ADD)
             nc.sync.dma_start(out=out_rows[:, cols], in_=result[:, cols])
+
+        for g in range(MAIN_PASSES, PASSES):
+            mx_pass(g, 0, left_tails[g - MAIN_PASSES][:])
+        finish(0)
+        for block in range(1, len(BLOCKS)):
+            first, width = BLOCKS[block]
+            mx_pass(PASSES - 2, block, right_before_last[:, first - N_TILE : first - N_TILE + width])
+        for block in range(1, len(BLOCKS)):
+            mx_pass(PASSES - 1, block, right_last[block - 1][:])
+            finish(block)

@@ -55,7 +55,7 @@ def tile_resampling_k_kernel(tc, encoded, W_words, W_scales, b, pos_emb, out):
         raws = []
         for a in range(SLABS):
             raw = raw_pool.tile([P, 4, 16, 64], BF16)
-            nc.sync.dma_start(out=raw[:].rearrange("p c r w -> p (c r w)"), in_=by_slab[a])
+            nc.scalar.dma_start(out=raw[:].rearrange("p c r w -> p (c r w)"), in_=by_slab[a])
             raws.append(raw)
         nc.sync.dma_start(out=table[0:BIG_PATCHES, :], in_=pos_emb)
         nc.sync.dma_start(out=table[BIG_PATCHES : BIG_PATCHES + 1, :], in_=b.unsqueeze(0))

import concourse.mybir as mybir
from concourse.masks import make_identity

F32 = mybir.dt.float32
BF16 = mybir.dt.bfloat16
I32 = mybir.dt.int32
U32 = mybir.dt.uint32
U8 = mybir.dt.uint8
FP8X4 = mybir.dt.float8_e4m3fn_x4
ADD = mybir.AluOpType.add

P = 128
IMAGES = 8
BIG_PATCHES = 16
F = 1024
K = 16384
K_PASS = 512
PASSES = K // K_PASS
N_TILE = 512
N_TILES = F // N_TILE
BLOCKS = ((0, 512), (512, 256), (768, 128), (896, 128))
LEFT = BLOCKS[0]
RIGHT = BLOCKS[1:]
SLABS = 4
SLAB_PASSES = PASSES // SLABS
SLAB_COLS = K // SLABS
PASSES_PER_LOAD = 2
TAIL_PASSES = 2
MAIN_PASSES = PASSES - TAIL_PASSES
PLANE_STARTS = 4
PLANE_SETS = PASSES // PLANE_STARTS

FLOPS = 2 * P * K * F


def tile_resampling_k_kernel(tc, encoded, W_words, W_scales, b, pos_emb, out):
    nc = tc.nc
    with (
        tc.tile_pool(name="const", bufs=1) as const,
        tc.tile_pool(name="raw", bufs=SLABS) as raw_pool,
        tc.tile_pool(name="stage", bufs=2) as stage,
        tc.tile_pool(name="weights", bufs=MAIN_PASSES // PASSES_PER_LOAD) as weights,
        tc.tile_pool(name="tail", bufs=1) as tail_pool,
        tc.psum_pool(name="acc", bufs=1) as acc_pool,
        tc.psum_pool(name="turned", bufs=4) as turned_pool,
    ):
        ident = const.tile([P, P], F32)
        make_identity(nc, ident[:])
        planes = const.tile([P, PLANE_SETS, F], U8, align_bytes=64)
        nc.vector.memset(planes[:].bitcast(I32), 0)
        table = const.tile([P, F], BF16)
        nc.vector.memset(table[:], 0.0)

        by_slab = encoded.rearrange("i (y a x c) d -> a (i y) x (c d)", y=4, a=SLABS, x=4, c=4)
        raws = []
        for a in range(SLABS):
            raw = raw_pool.tile([P, 4, 16, 64], BF16)
            nc.scalar.dma_start(out=raw[:].rearrange("p c r w -> p (c r w)"), in_=by_slab[a])
            raws.append(raw)
        nc.sync.dma_start(out=table[0:BIG_PATCHES, :], in_=pos_emb)
        nc.sync.dma_start(out=table[BIG_PATCHES : BIG_PATCHES + 1, :], in_=b.unsqueeze(0))
        for G in range(PLANE_SETS):
            for Q in range(4):
                nc.gpsimd.dma_start(
                    out=planes[32 * Q : 32 * Q + 16, G, :].bitcast(F32),
                    in_=W_scales[4 * G : 4 * G + 4, 4 * Q : 4 * Q + 4, :].bitcast(F32),
                )
        w_tiles = []
        for g0 in range(0, MAIN_PASSES, PASSES_PER_LOAD):
            w = weights.tile([P, PASSES_PER_LOAD, F], U32, align_bytes=64)
            nc.sync.dma_start(
                out=w[:].bitcast(I32),
                in_=W_words[g0 : g0 + PASSES_PER_LOAD].rearrange("g p n t -> p g (n t)").bitcast(I32),
            )
            w_tiles.append(w)
        def load_tail(g, first, width):
            w_tail = tail_pool.tile([P, width], U32, align_bytes=64, name="tail_%d_%d" % (g, first))
            nc.sync.dma_start(
                out=w_tail[:].bitcast(I32),
                in_=W_words[g].rearrange("p n t -> p (n t)").bitcast(I32)[:, first : first + width],
            )
            return w_tail

        left_tails = [load_tail(g, LEFT[0], LEFT[1]) for g in range(MAIN_PASSES, PASSES)]
        right_before_last = load_tail(PASSES - 2, N_TILE, N_TILE)
        right_last = [load_tail(PASSES - 1, first, width) for first, width in RIGHT]

        select = const.tile([P, IMAGES, BIG_PATCHES], BF16)
        nc.vector.tensor_scalar(
            out=select[:],
            in0=ident[:, 0:BIG_PATCHES].unsqueeze(1).to_broadcast([P, IMAGES, BIG_PATCHES]),
            scalar1=ident[:, BIG_PATCHES : BIG_PATCHES + 1],
            scalar2=None,
            op0=ADD,
        )
        addend = const.tile([P, F], F32)
        for h in range(N_TILES):
            cols = slice(h * N_TILE, (h + 1) * N_TILE)
            turned = turned_pool.tile([P, N_TILE], F32)
            nc.tensor.matmul(
                out=turned[:],
                lhsT=select[:].rearrange("p i j -> p (i j)"),
                rhs=table[:, cols],
                start=True,
                stop=True,
            )
            nc.scalar.copy(out=addend[:, cols], in_=turned[:])

        x_codes = const.tile([P, PASSES, P], U32, align_bytes=64)
        x_scales = const.tile([P, PASSES, P], U8, align_bytes=64)
        for a in range(SLABS):
            ordered = stage.tile([P, 16, 4, 64], BF16)
            nc.scalar.copy(out=ordered[:].bitcast(F32), in_=raws[a][:].bitcast(F32).rearrange("p c r w -> p r c w"))
            words = ordered[:].rearrange("p r c w -> p (r c w)").bitcast(F32)
            grouped = stage.tile([P, SLAB_PASSES, P, 4], BF16, align_bytes=64)
            grouped_words = grouped[:].bitcast(F32)
            for pair in range(SLAB_PASSES // 2):
                turned = turned_pool.tile([P, 2, 2, P], F32)
                for j in range(2):
                    first = 256 * (2 * pair + j)
                    for u in range(2):
                        nc.tensor.transpose(turned[:, j, u, :], words[:, first + u : first + 256 : 2], ident[:])
                nc.vector.tensor_copy(
                    out=grouped_words[:, 2 * pair : 2 * pair + 2, :, :],
                    in_=turned[:].rearrange("p j u m -> p j m u"),
                )
            slab = slice(a * SLAB_PASSES, (a + 1) * SLAB_PASSES)
            nc.vector.quantize_mx(
                out=x_codes[:, slab, :].rearrange("p g m -> p (g m)").bitcast(FP8X4),
                scales=x_scales[:, slab, :].rearrange("p g m -> p (g m)"),
                in_=grouped[:].rearrange("p g m t -> p (g m t)"),
            )

        accs = [acc_pool.tile([P, width], F32, name="acc%d" % first) for first, width in BLOCKS]

        def mx_pass(g, block, w_words):
            first, width = BLOCKS[block]
            nc.tensor.matmul_mx(
                out=accs[block][:],
                lhsT=x_codes[:, g, :].bitcast(FP8X4),
                lhsT_scale=x_scales[:, g, :],
                rhs=w_words.bitcast(FP8X4),
                rhs_scale=planes[4 * (g % PLANE_STARTS) : P, g // PLANE_STARTS, first : first + width],
                start=(g == 0),
                stop=(g == PASSES - 1),
            )

        for g in range(MAIN_PASSES):
            for block, (first, width) in enumerate(BLOCKS):
                mx_pass(g, block, w_tiles[g // PASSES_PER_LOAD][:, g % PASSES_PER_LOAD, first : first + width])

        out_rows = out.flatten_outer_dims()
        result = const.tile([P, F], F32)

        def finish(block):
            first, width = BLOCKS[block]
            cols = slice(first, first + width)
            nc.vector.tensor_tensor(out=result[:, cols], in0=accs[block][:], in1=addend[:, cols], op=ADD)
            nc.sync.dma_start(out=out_rows[:, cols], in_=result[:, cols])

        for g in range(MAIN_PASSES, PASSES):
            mx_pass(g, 0, left_tails[g - MAIN_PASSES][:])
        finish(0)
        for block in range(1, len(BLOCKS)):
            first, width = BLOCKS[block]
            mx_pass(PASSES - 2, block, right_before_last[:, first - N_TILE : first - N_TILE + width])
        for block in range(1, len(BLOCKS)):
            mx_pass(PASSES - 1, block, right_last[block - 1][:])
            finish(block)
